import numpy as np
import ml_dtypes


def mxq(x, axis, fmt="e4m3"):
    dtype, down = {"e4m3": (ml_dtypes.float8_e4m3fn, 7), "e5m2": (ml_dtypes.float8_e5m2, 14)}[fmt]
    v = np.moveaxis(np.asarray(x, np.float32).astype(ml_dtypes.bfloat16).astype(np.float64), axis, -1)
    blocks = v.reshape(v.shape[:-1] + (-1, 32))
    amax = np.abs(blocks).max(-1, keepdims=True)
    byte = np.maximum(np.where(amax > 0, np.frexp(amax)[1] - 1 + 127, 0) - down, 1)
    scale = np.exp2(byte - 127.0)
    codes = (blocks / scale).astype(np.float32).astype(dtype).astype(np.float64)
    return np.moveaxis((codes * scale).reshape(v.shape), -1, axis)


WIDE = False


def mx_kscale(k):
    if not WIDE:
        return np.ones(k)
    levels = np.array([10, -10, 5, -5, 0])
    if k % 512:
        return np.exp2(np.random.permutation(np.resize(levels, k // 32))).repeat(32)
    a = np.empty((k // 512, 16))
    for p in range(k // 512):
        a[p, :8] = np.random.permutation(np.resize(levels, 8))
        for g in range(8):
            far = levels[np.abs(levels - a[p, g]) >= 10]
            a[p, g + 8] = far[np.random.randint(len(far))]
    return np.exp2(a.ravel()).repeat(32)


BF16 = ml_dtypes.bfloat16


def bf(x):
    return np.asarray(x, np.float32).astype(BF16)


def f64(x):
    return np.asarray(x).astype(np.float64)


B, S, D_IN, D_OUT = 2, 4096, 1024, 256


def quant8(w):
    mv = np.max(np.abs(w))
    q = np.ceil(np.log2(mv)) - 6.0
    scale = np.exp2(q)
    return np.round(w / scale) * scale


def setup_inputs():
    s = mx_kscale(D_IN)
    x = np.random.standard_normal((B, S, D_IN))
    weight = np.random.standard_normal((D_OUT, D_IN)) * 3.0 / np.sqrt(D_IN)
    w_upper = quant8(weight)
    w_lower = weight - w_upper
    return {"x": bf(x * s), "weight_upper": bf(w_upper / s[None, :]), "weight_lower": bf(w_lower / s[None, :])}


def reference(x, weight_upper, weight_lower):
    xq = mxq(f64(x), 2, "e4m3")
    y_upper = xq @ mxq(f64(weight_upper), 1, "e4m3").T
    y_lower = xq @ mxq(f64(weight_lower), 1, "e4m3").T
    return y_upper + y_lower

@@ -1,0 +1,189 @@
+from contextlib import ExitStack
+
+import concourse.mybir as mybir
+from concourse.masks import make_identity
+
+BF16 = mybir.dt.bfloat16
+F32 = mybir.dt.float32
+U32 = mybir.dt.uint32
+U8 = mybir.dt.uint8
+FP8X4 = mybir.dt.float8_e4m3fn_x4
+
+P = 128
+K = 1024
+N_OUT = 256
+TOKENS = 8192
+N_TILES = TOKENS // P
+CHUNK = 4
+N_CHUNKS = N_TILES // CHUNK
+AHEAD = 8
+GROUP = 4
+T_BUFS = 4
+A_BUFS = 4
+EARLY_Q = 4
+
+FLOPS = 2 * 2 * TOKENS * K * N_OUT
+
+
+def tile_virtual16bmatmul_t_kernel(tc, x, weight_upper, weight_lower, out):
+    nc = tc.nc
+    xf = x.flatten_outer_dims()
+    of = out.flatten_outer_dims()
+
+    with ExitStack() as ctx:
+        const = ctx.enter_context(tc.tile_pool(name="const", bufs=1))
+        wraw_pool = ctx.enter_context(tc.tile_pool(name="wrawp", bufs=4))
+        x_pool = ctx.enter_context(tc.tile_pool(name="xp", bufs=N_CHUNKS))
+        g_pool = ctx.enter_context(tc.tile_pool(name="gp", bufs=8))
+        c_pool = ctx.enter_context(tc.tile_pool(name="cp", bufs=16))
+        o_pool = ctx.enter_context(tc.tile_pool(name="op", bufs=6))
+        t_psum = ctx.enter_context(tc.psum_pool(name="tps", bufs=T_BUFS))
+        a_psum = ctx.enter_context(tc.psum_pool(name="aps", bufs=A_BUFS))
+        ctx.enter_context(tc.manual_schedule())
+
+        ident = const.tile([P, P], F32, name="ident")
+        make_identity(nc, ident[:])
+
+        w_raw = []
+        for wi, w_src in enumerate((weight_upper, weight_lower)):
+            for h in range(2):
+                wr = wraw_pool.tile([P, K], BF16, name="wraw%d" % (2 * wi + h), tag="wraw")
+                nc.sync.dma_start(out=wr[:], in_=w_src[P * h : P * (h + 1), :])
+                w_raw.append(wr)
+
+        x_chunks = {}
+
+        def load_chunk(c, pieces):
+            xc = x_pool.tile([P, CHUNK * K], BF16, name="xc%d" % c, tag="xc")
+            src = xf[CHUNK * P * c : CHUNK * P * (c + 1), :].rearrange("(p t) k -> p (t k)", t=CHUNK)
+            step = CHUNK * K // pieces
+            for i in range(pieces):
+                nc.sync.dma_start(out=xc[:, step * i : step * (i + 1)], in_=src[:, step * i : step * (i + 1)])
+            x_chunks[c] = xc
+
+        load_chunk(0, 4)
+        load_chunk(1, 2)
+        for c in range(2, AHEAD):
+            load_chunk(c, 1)
+
+        warm_src = const.tile([P, 512], BF16, name="warm_src")
+        nc.vector.memset(warm_src[:], 0.0)
+        warm_bank = a_psum.tile([P, 512], F32, name="warm_bank", tag="acc")
+
+        def keep_warm(n):
+            for rep in range(n):
+                nc.tensor.matmul(out=warm_bank[:], lhsT=warm_src[:, 0:P], rhs=warm_src[:], start=True, stop=True)
+
+        keep_warm(6)
+
+        def transpose_words(bank, words):
+            for c in range(4):
+                first = 2 * P * (c // 2) + c % 2
+                nc.tensor.transpose(bank[:, c, :], words[:, first : 2 * P * (c // 2 + 1) : 2], ident[:])
+
+        w_codes = []
+        w_scales = []
+        for wi in range(2):
+            wg = const.tile([P, 4 * 2 * N_OUT], BF16, name="wg%d" % wi, align_bytes=64)
+            wg_words = wg[:].bitcast(F32).rearrange("p (g n u) -> p g n u", g=2, u=2)
+            for h in range(2):
+                wt = t_psum.tile([P, 4, P], F32, name="wt%d" % (2 * wi + h), tag="xt")
+                transpose_words(wt, w_raw[2 * wi + h][:].bitcast(F32))
+                keep_warm(1)
+                nc.scalar.copy(
+                    out=wg_words[:, :, P * h : P * (h + 1), :],
+                    in_=wt[:].rearrange("p (g u) r -> p g r u", u=2),
+                )
+            wc = const.tile([P, 2 * N_OUT], U32, name="wc%d" % wi, align_bytes=64)
+            ws = const.tile([P, 2 * N_OUT], U8, name="ws%d" % wi, align_bytes=64)
+            nc.vector.quantize_mx(out=wc[:].bitcast(FP8X4), scales=ws[:], in_=wg[:])
+            w_codes.append(wc)
+            w_scales.append(ws)
+
+        grouped = {}
+        x_codes = {}
+        x_scales = {}
+        acc = {}
+        o_tiles = {}
+
+        def transpose_tile(i):
+            words = x_chunks[i // CHUNK][:].bitcast(F32)
+            t = i % CHUNK
+            xt = t_psum.tile([P, 4, P], F32, name="xt%d" % i, tag="xt")
+            transpose_words(xt, words[:, (K // 2) * t : (K // 2) * (t + 1)])
+            if i < 3:
+                keep_warm(1)
+            gr = g_pool.tile([P, K], BF16, name="gr%d" % i, tag="gr", align_bytes=64)
+            nc.scalar.copy(
+                out=gr[:].bitcast(F32).rearrange("p (g r u) -> p g r u", g=2, u=2),
+                in_=xt[:].rearrange("p (g u) r -> p g r u", u=2),
+            )
+            grouped[i] = gr
+
+        def quantise_tile(i):
+            xcod = c_pool.tile([P, K // 4], U32, name="xcod%d" % i, tag="xcod", align_bytes=64)
+            xsca = c_pool.tile([P, K // 4], U8, name="xsca%d" % i, tag="xsca", align_bytes=64)
+            nc.vector.quantize_mx(out=xcod[:].bitcast(FP8X4), scales=xsca[:], in_=grouped[i][:])
+            x_codes[i] = xcod
+            x_scales[i] = xsca
+
+        def multiply_tile(i):
+            pair = i // 2
+            c = i // CHUNK
+            alone = i >= N_TILES - 2
+            if i % 2 == 0 or alone:
+                acc[pair] = a_psum.tile([P, 2, N_OUT], F32, name="acc%d" % i, tag="acc")
+            if i % CHUNK == 0:
+                o_tiles[c] = o_pool.tile([P, CHUNK * N_OUT], F32, name="osb%d" % c, tag="osb")
+            n_pass = 0
+            for g in range(2):
+                for wi in range(2):
+                    nc.tensor.matmul_mx(
+                        out=acc[pair][:, 0 if alone else i % 2, :],
+                        lhsT=x_codes[i][:, P * g : P * (g + 1)].bitcast(FP8X4),
+                        lhsT_scale=x_scales[i][:, P * g : P * (g + 1)],
+                        rhs=w_codes[wi][:, N_OUT * g : N_OUT * (g + 1)].bitcast(FP8X4),
+                        rhs_scale=w_scales[wi][:, N_OUT * g : N_OUT * (g + 1)],
+                        start=(n_pass == 0),
+                        stop=(n_pass == 3),
+                    )
+                    n_pass += 1
+            dst = of[CHUNK * P * c : CHUNK * P * (c + 1), :].rearrange("(p t) n -> p (t n)", t=CHUNK)
+            if alone:
+                cols = slice(N_OUT * (i % CHUNK), N_OUT * (i % CHUNK + 1))
+                if i % 2 == 0:
+                    nc.scalar.copy(out=o_tiles[c][:, cols], in_=acc[pair][:, 0, :])
+                else:
+                    nc.vector.tensor_copy(out=o_tiles[c][:, cols], in_=acc[pair][:, 0, :])
+                nc.sync.dma_start(out=dst[:, cols], in_=o_tiles[c][:, cols])
+            elif i % 2 == 1:
+                b = pair % 2
+                cols = slice(2 * N_OUT * b, 2 * N_OUT * (b + 1))
+                nc.vector.tensor_copy(out=o_tiles[c][:, cols], in_=acc[pair][:].rearrange("p h n -> p (h n)"))
+                if c == N_CHUNKS - 1:
+                    nc.sync.dma_start(out=dst[:, cols], in_=o_tiles[c][:, cols])
+                elif b == 1:
+                    nc.sync.dma_start(out=dst, in_=o_tiles[c][:])
+                    if c + AHEAD < N_CHUNKS:
+                        load_chunk(c + AHEAD, 1)
+
+        groups = [[0, 1], [2, 3]] + [list(range(s, s + GROUP)) for s in range(4, N_TILES, GROUP)]
+        for i in groups[0]:
+            transpose_tile(i)
+        for i in groups[0]:
+            quantise_tile(i)
+        for k in range(len(groups)):
+            following = groups[k + 1] if k + 1 < len(groups) else []
+            for i in following:
+                transpose_tile(i)
+            for i in following[:EARLY_Q]:
+                quantise_tile(i)
+            late = following[EARLY_Q:]
+            for n, i in enumerate(groups[k]):
+                multiply_tile(i)
+                if n == 1:
+                    for j in late:
+                        quantise_tile(j)
+            if len(groups[k]) < 2:
+                for j in late:
+                    quantise_tile(j)

@@ -20,7 +20,6 @@ AHEAD = 8
 GROUP = 4
 T_BUFS = 4
 A_BUFS = 4
-EARLY_Q = 4
 
 FLOPS = 2 * 2 * TOKENS * K * N_OUT
 
@@ -34,6 +33,8 @@ def tile_virtual16bmatmul_t_kernel(tc, x, weight_upper, weight_lower, out):
         const = ctx.enter_context(tc.tile_pool(name="const", bufs=1))
         wraw_pool = ctx.enter_context(tc.tile_pool(name="wrawp", bufs=4))
         x_pool = ctx.enter_context(tc.tile_pool(name="xp", bufs=N_CHUNKS))
+        r_pool = ctx.enter_context(tc.tile_pool(name="rp", bufs=4))
+        wr_pool = ctx.enter_context(tc.tile_pool(name="wrp", bufs=4))
         g_pool = ctx.enter_context(tc.tile_pool(name="gp", bufs=8))
         c_pool = ctx.enter_context(tc.tile_pool(name="cp", bufs=16))
         o_pool = ctx.enter_context(tc.tile_pool(name="op", bufs=6))
@@ -76,11 +77,22 @@ def tile_virtual16bmatmul_t_kernel(tc, x, weight_upper, weight_lower, out):
 
         keep_warm(6)
 
-        def transpose_words(bank, words):
-            for c in range(4):
-                first = 2 * P * (c // 2) + c % 2
-                nc.tensor.transpose(bank[:, c, :], words[:, first : 2 * P * (c // 2 + 1) : 2], ident[:])
+        def reorder(dst, src):
+            nc.vector.tensor_copy(
+                out=dst.rearrange("p (u b i) -> p u b i", u=2, i=16),
+                in_=src.rearrange("p (b u i) -> p u b i", u=2, i=16),
+            )
 
+        def transpose_words(bank, words, tiles, t):
+            for c in range(4):
+                first = (c % 2) * (2 * P * tiles) + 2 * P * t + P * (c // 2)
+                nc.tensor.transpose(bank[:, c, :], words[:, first : first + P], ident[:])
+
+        w_re = []
+        for h in range(4):
+            wre = wr_pool.tile([P, K], BF16, name="wre%d" % h, tag="wre")
+            reorder(wre[:], w_raw[h][:])
+            w_re.append(wre)
         w_codes = []
         w_scales = []
         for wi in range(2):
@@ -88,7 +100,7 @@ def tile_virtual16bmatmul_t_kernel(tc, x, weight_upper, weight_lower, out):
             wg_words = wg[:].bitcast(F32).rearrange("p (g n u) -> p g n u", g=2, u=2)
             for h in range(2):
                 wt = t_psum.tile([P, 4, P], F32, name="wt%d" % (2 * wi + h), tag="xt")
-                transpose_words(wt, w_raw[2 * wi + h][:].bitcast(F32))
+                transpose_words(wt, w_re[2 * wi + h][:].bitcast(F32), 1, 0)
                 keep_warm(1)
                 nc.scalar.copy(
                     out=wg_words[:, :, P * h : P * (h + 1), :],
@@ -100,17 +112,22 @@ def tile_virtual16bmatmul_t_kernel(tc, x, weight_upper, weight_lower, out):
             w_codes.append(wc)
             w_scales.append(ws)
 
+        reordered = {}
         grouped = {}
         x_codes = {}
         x_scales = {}
         acc = {}
         o_tiles = {}
 
+        def reorder_pair(j):
+            half = j % (CHUNK // 2)
+            re = r_pool.tile([P, 2 * K], BF16, name="re%d" % j, tag="re")
+            reorder(re[:], x_chunks[2 * j // CHUNK][:, 2 * K * half : 2 * K * (half + 1)])
+            reordered[j] = re
+
         def transpose_tile(i):
-            words = x_chunks[i // CHUNK][:].bitcast(F32)
-            t = i % CHUNK
             xt = t_psum.tile([P, 4, P], F32, name="xt%d" % i, tag="xt")
-            transpose_words(xt, words[:, (K // 2) * t : (K // 2) * (t + 1)])
+            transpose_words(xt, reordered[i // 2][:].bitcast(F32), 2, i % 2)
             if i < 3:
                 keep_warm(1)
             gr = g_pool.tile([P, K], BF16, name="gr%d" % i, tag="gr", align_bytes=64)
@@ -159,7 +176,10 @@ def tile_virtual16bmatmul_t_kernel(tc, x, weight_upper, weight_lower, out):
             elif i % 2 == 1:
                 b = pair % 2
                 cols = slice(2 * N_OUT * b, 2 * N_OUT * (b + 1))
-                nc.vector.tensor_copy(out=o_tiles[c][:, cols], in_=acc[pair][:].rearrange("p h n -> p (h n)"))
+                if b == 0:
+                    nc.scalar.copy(out=o_tiles[c][:, cols], in_=acc[pair][:].rearrange("p h n -> p (h n)"))
+                else:
+                    nc.vector.tensor_copy(out=o_tiles[c][:, cols], in_=acc[pair][:].rearrange("p h n -> p (h n)"))
                 if c == N_CHUNKS - 1:
                     nc.sync.dma_start(out=dst[:, cols], in_=o_tiles[c][:, cols])
                 elif b == 1:
@@ -168,22 +188,20 @@ def tile_virtual16bmatmul_t_kernel(tc, x, weight_upper, weight_lower, out):
                         load_chunk(c + AHEAD, 1)
 
         groups = [[0, 1], [2, 3]] + [list(range(s, s + GROUP)) for s in range(4, N_TILES, GROUP)]
+        for j in range(2):
+            reorder_pair(j)
         for i in groups[0]:
             transpose_tile(i)
         for i in groups[0]:
             quantise_tile(i)
         for k in range(len(groups)):
+            for i in groups[k + 2] if k + 2 < len(groups) else []:
+                if i % 2 == 0:
+                    reorder_pair(i // 2)
             following = groups[k + 1] if k + 1 < len(groups) else []
             for i in following:
                 transpose_tile(i)
-            for i in following[:EARLY_Q]:
+            for i in following:
                 quantise_tile(i)
-            late = following[EARLY_Q:]
-            for n, i in enumerate(groups[k]):
+            for i in groups[k]:
                 multiply_tile(i)
-                if n == 1:
-                    for j in late:
-                        quantise_tile(j)
-            if len(groups[k]) < 2:
-                for j in late:
-                    quantise_tile(j)

@@ -75,7 +75,7 @@ def tile_virtual16bmatmul_t_kernel(tc, x, weight_upper, weight_lower, out):
             for rep in range(n):
                 nc.tensor.matmul(out=warm_bank[:], lhsT=warm_src[:, 0:P], rhs=warm_src[:], start=True, stop=True)
 
-        keep_warm(6)
+        keep_warm(4)
 
         def reorder(dst, src):
             nc.vector.tensor_copy(
@@ -88,30 +88,6 @@ def tile_virtual16bmatmul_t_kernel(tc, x, weight_upper, weight_lower, out):
                 first = (c % 2) * (2 * P * tiles) + 2 * P * t + P * (c // 2)
                 nc.tensor.transpose(bank[:, c, :], words[:, first : first + P], ident[:])
 
-        w_re = []
-        for h in range(4):
-            wre = wr_pool.tile([P, K], BF16, name="wre%d" % h, tag="wre")
-            reorder(wre[:], w_raw[h][:])
-            w_re.append(wre)
-        w_codes = []
-        w_scales = []
-        for wi in range(2):
-            wg = const.tile([P, 4 * 2 * N_OUT], BF16, name="wg%d" % wi, align_bytes=64)
-            wg_words = wg[:].bitcast(F32).rearrange("p (g n u) -> p g n u", g=2, u=2)
-            for h in range(2):
-                wt = t_psum.tile([P, 4, P], F32, name="wt%d" % (2 * wi + h), tag="xt")
-                transpose_words(wt, w_re[2 * wi + h][:].bitcast(F32), 1, 0)
-                keep_warm(1)
-                nc.scalar.copy(
-                    out=wg_words[:, :, P * h : P * (h + 1), :],
-                    in_=wt[:].rearrange("p (g u) r -> p g r u", u=2),
-                )
-            wc = const.tile([P, 2 * N_OUT], U32, name="wc%d" % wi, align_bytes=64)
-            ws = const.tile([P, 2 * N_OUT], U8, name="ws%d" % wi, align_bytes=64)
-            nc.vector.quantize_mx(out=wc[:].bitcast(FP8X4), scales=ws[:], in_=wg[:])
-            w_codes.append(wc)
-            w_scales.append(ws)
-
         reordered = {}
         grouped = {}
         x_codes = {}
@@ -119,15 +95,17 @@ def tile_virtual16bmatmul_t_kernel(tc, x, weight_upper, weight_lower, out):
         acc = {}
         o_tiles = {}
 
-        def reorder_pair(j):
-            half = j % (CHUNK // 2)
-            re = r_pool.tile([P, 2 * K], BF16, name="re%d" % j, tag="re")
-            reorder(re[:], x_chunks[2 * j // CHUNK][:, 2 * K * half : 2 * K * (half + 1)])
-            reordered[j] = re
+        def reorder_tiles(i, n):
+            t = i % CHUNK
+            re = r_pool.tile([P, 2 * K], BF16, name="re%d" % i, tag="re")
+            reorder(re[:, 0 : n * K], x_chunks[i // CHUNK][:, K * t : K * (t + n)])
+            for s in range(n):
+                reordered[i + s] = (re, n, s)
 
         def transpose_tile(i):
             xt = t_psum.tile([P, 4, P], F32, name="xt%d" % i, tag="xt")
-            transpose_words(xt, reordered[i // 2][:].bitcast(F32), 2, i % 2)
+            re, n, s = reordered[i]
+            transpose_words(xt, re[:, 0 : n * K].bitcast(F32), n, s)
             if i < 3:
                 keep_warm(1)
             gr = g_pool.tile([P, K], BF16, name="gr%d" % i, tag="gr", align_bytes=64)
@@ -187,21 +165,66 @@ def tile_virtual16bmatmul_t_kernel(tc, x, weight_upper, weight_lower, out):
                     if c + AHEAD < N_CHUNKS:
                         load_chunk(c + AHEAD, 1)
 
+        w_re = []
+        w_grouped = []
+        w_codes = []
+        w_scales = []
+        for h in range(4):
+            wre = wr_pool.tile([P, K], BF16, name="wre%d" % h, tag="wre")
+            reorder(wre[:], w_raw[h][:])
+            w_re.append(wre)
+
+        def transpose_weight(wi):
+            wg = const.tile([P, 4 * 2 * N_OUT], BF16, name="wg%d" % wi, align_bytes=64)
+            wg_words = wg[:].bitcast(F32).rearrange("p (g n u) -> p g n u", g=2, u=2)
+            for h in range(2):
+                wt = t_psum.tile([P, 4, P], F32, name="wt%d" % (2 * wi + h), tag="xt")
+                transpose_words(wt, w_re[2 * wi + h][:].bitcast(F32), 1, 0)
+                keep_warm(1)
+                (nc.vector.tensor_copy if (wi, h) == (0, 1) else nc.scalar.copy)(
+                    out=wg_words[:, :, P * h : P * (h + 1), :],
+                    in_=wt[:].rearrange("p (g u) r -> p g r u", u=2),
+                )
+            w_grouped.append(wg)
+
+        def quantise_weight(wi):
+            wc = const.tile([P, 2 * N_OUT], U32, name="wc%d" % wi, align_bytes=64)
+            ws = const.tile([P, 2 * N_OUT], U8, name="ws%d" % wi, align_bytes=64)
+            nc.vector.quantize_mx(out=wc[:].bitcast(FP8X4), scales=ws[:], in_=w_grouped[wi][:])
+            w_codes.append(wc)
+            w_scales.append(ws)
+
         groups = [[0, 1], [2, 3]] + [list(range(s, s + GROUP)) for s in range(4, N_TILES, GROUP)]
-        for j in range(2):
-            reorder_pair(j)
+        transpose_weight(0)
+        for i in groups[0]:
+            reorder_tiles(i, 1)
+        transpose_weight(1)
+        quantise_weight(0)
+        reorder_tiles(2, 2)
         for i in groups[0]:
             transpose_tile(i)
+        quantise_weight(1)
         for i in groups[0]:
             quantise_tile(i)
         for k in range(len(groups)):
-            for i in groups[k + 2] if k + 2 < len(groups) else []:
-                if i % 2 == 0:
-                    reorder_pair(i // 2)
             following = groups[k + 1] if k + 1 < len(groups) else []
+            ahead = groups[k + 2] if k + 2 < len(groups) else []
             for i in following:
                 transpose_tile(i)
-            for i in following:
-                quantise_tile(i)
+            pairs = ahead[::2]
+            if len(following) == GROUP:
+                quantise_tile(following[0])
+                for i in pairs[:1]:
+                    reorder_tiles(i, 2)
+                quantise_tile(following[1])
+                quantise_tile(following[2])
+                for i in pairs[1:]:
+                    reorder_tiles(i, 2)
+                quantise_tile(following[3])
+            else:
+                for n, i in enumerate(following):
+                    for j in pairs[n : n + 1]:
+                        reorder_tiles(j, 2)
+                    quantise_tile(i)
             for i in groups[k]:
                 multiply_tile(i)

@@ -37,6 +37,7 @@ def tile_virtual16bmatmul_t_kernel(tc, x, weight_upper, weight_lower, out):
         wr_pool = ctx.enter_context(tc.tile_pool(name="wrp", bufs=4))
         g_pool = ctx.enter_context(tc.tile_pool(name="gp", bufs=8))
         c_pool = ctx.enter_context(tc.tile_pool(name="cp", bufs=16))
+        l_pool = ctx.enter_context(tc.tile_pool(name="lp", bufs=4))
         o_pool = ctx.enter_context(tc.tile_pool(name="op", bufs=6))
         t_psum = ctx.enter_context(tc.psum_pool(name="tps", bufs=T_BUFS))
         a_psum = ctx.enter_context(tc.psum_pool(name="aps", bufs=A_BUFS))
@@ -92,7 +93,6 @@ def tile_virtual16bmatmul_t_kernel(tc, x, weight_upper, weight_lower, out):
         grouped = {}
         x_codes = {}
         x_scales = {}
-        acc = {}
         o_tiles = {}
 
         def reorder_tiles(i, n):
@@ -123,52 +123,45 @@ def tile_virtual16bmatmul_t_kernel(tc, x, weight_upper, weight_lower, out):
             x_scales[i] = xsca
 
         def multiply_tile(i):
-            pair = i // 2
             c = i // CHUNK
-            alone = i >= N_TILES - 2
-            if i % 2 == 0 or alone:
-                acc[pair] = a_psum.tile([P, 2, N_OUT], F32, name="acc%d" % i, tag="acc")
-            if i % CHUNK == 0:
+            t = i % CHUNK
+            last = i >= N_TILES - 2
+            bank = a_psum.tile([P, 2, N_OUT], F32, name="acc%d" % i, tag="acc")
+            if t == 0:
                 o_tiles[c] = o_pool.tile([P, CHUNK * N_OUT], F32, name="osb%d" % c, tag="osb")
-            n_pass = 0
-            for g in range(2):
-                for wi in range(2):
-                    nc.tensor.matmul_mx(
-                        out=acc[pair][:, 0 if alone else i % 2, :],
-                        lhsT=x_codes[i][:, P * g : P * (g + 1)].bitcast(FP8X4),
-                        lhsT_scale=x_scales[i][:, P * g : P * (g + 1)],
-                        rhs=w_codes[wi][:, N_OUT * g : N_OUT * (g + 1)].bitcast(FP8X4),
-                        rhs_scale=w_scales[wi][:, N_OUT * g : N_OUT * (g + 1)],
-                        start=(n_pass == 0),
-                        stop=(n_pass == 3),
-                    )
-                    n_pass += 1
+            cols = slice(N_OUT * t, N_OUT * (t + 1))
             dst = of[CHUNK * P * c : CHUNK * P * (c + 1), :].rearrange("(p t) n -> p (t n)", t=CHUNK)
-            if alone:
-                cols = slice(N_OUT * (i % CHUNK), N_OUT * (i % CHUNK + 1))
-                if i % 2 == 0:
-                    nc.scalar.copy(out=o_tiles[c][:, cols], in_=acc[pair][:, 0, :])
-                else:
-                    nc.vector.tensor_copy(out=o_tiles[c][:, cols], in_=acc[pair][:, 0, :])
+            width = N_OUT if last else 2 * N_OUT
+            starts = [(g, n) for g in range(2) for n in range(0, 2 * N_OUT, width)]
+            for n_pass, (g, n) in enumerate(starts):
+                w_cols = slice(2 * N_OUT * g + n, 2 * N_OUT * g + n + width)
+                nc.tensor.matmul_mx(
+                    out=bank[:].rearrange("p h n -> p (h n)")[:, 0:width],
+                    lhsT=x_codes[i][:, P * g : P * (g + 1)].bitcast(FP8X4),
+                    lhsT_scale=x_scales[i][:, P * g : P * (g + 1)],
+                    rhs=w_codes[:, w_cols].bitcast(FP8X4),
+                    rhs_scale=w_scales[:, w_cols],
+                    start=(n_pass == 0),
+                    stop=(n_pass == len(starts) - 1),
+                )
+            if last:
+                (nc.scalar.copy if t % 2 == 0 else nc.vector.tensor_copy)(out=o_tiles[c][:, cols], in_=bank[:, 0, :])
                 nc.sync.dma_start(out=dst[:, cols], in_=o_tiles[c][:, cols])
-            elif i % 2 == 1:
-                b = pair % 2
-                cols = slice(2 * N_OUT * b, 2 * N_OUT * (b + 1))
-                if b == 0:
-                    nc.scalar.copy(out=o_tiles[c][:, cols], in_=acc[pair][:].rearrange("p h n -> p (h n)"))
-                else:
-                    nc.vector.tensor_copy(out=o_tiles[c][:, cols], in_=acc[pair][:].rearrange("p h n -> p (h n)"))
-                if c == N_CHUNKS - 1:
-                    nc.sync.dma_start(out=dst[:, cols], in_=o_tiles[c][:, cols])
-                elif b == 1:
-                    nc.sync.dma_start(out=dst, in_=o_tiles[c][:])
-                    if c + AHEAD < N_CHUNKS:
-                        load_chunk(c + AHEAD, 1)
+                return
+            low = l_pool.tile([P, N_OUT], F32, name="low%d" % i, tag="low")
+            nc.scalar.copy(out=low[:], in_=bank[:, 1, :])
+            nc.vector.tensor_tensor(out=o_tiles[c][:, cols], in0=bank[:, 0, :], in1=low[:], op=mybir.AluOpType.add)
+            if c == N_CHUNKS - 1 and t == 1:
+                nc.sync.dma_start(out=dst[:, 0 : 2 * N_OUT], in_=o_tiles[c][:, 0 : 2 * N_OUT])
+            elif t == CHUNK - 1:
+                nc.sync.dma_start(out=dst, in_=o_tiles[c][:])
+                if c + AHEAD < N_CHUNKS:
+                    load_chunk(c + AHEAD, 1)
 
         w_re = []
         w_grouped = []
-        w_codes = []
-        w_scales = []
+        w_codes = const.tile([P, 4 * N_OUT], U32, name="w_codes", align_bytes=64)
+        w_scales = const.tile([P, 4 * N_OUT], U8, name="w_scales", align_bytes=64)
         for h in range(4):
             wre = wr_pool.tile([P, K], BF16, name="wre%d" % h, tag="wre")
             reorder(wre[:], w_raw[h][:])
@@ -188,11 +181,13 @@ def tile_virtual16bmatmul_t_kernel(tc, x, weight_upper, weight_lower, out):
             w_grouped.append(wg)
 
         def quantise_weight(wi):
-            wc = const.tile([P, 2 * N_OUT], U32, name="wc%d" % wi, align_bytes=64)
-            ws = const.tile([P, 2 * N_OUT], U8, name="ws%d" % wi, align_bytes=64)
-            nc.vector.quantize_mx(out=wc[:].bitcast(FP8X4), scales=ws[:], in_=w_grouped[wi][:])
-            w_codes.append(wc)
-            w_scales.append(ws)
+            for g in range(2):
+                w_cols = slice(N_OUT * (2 * g + wi), N_OUT * (2 * g + wi + 1))
+                nc.vector.quantize_mx(
+                    out=w_codes[:, w_cols].bitcast(FP8X4),
+                    scales=w_scales[:, w_cols],
+                    in_=w_grouped[wi][:, 4 * N_OUT * g : 4 * N_OUT * (g + 1)],
+                )
 
         groups = [[0, 1], [2, 3]] + [list(range(s, s + GROUP)) for s in range(4, N_TILES, GROUP)]
         transpose_weight(0)

from contextlib import ExitStack

import concourse.mybir as mybir
from concourse.masks import make_identity

BF16 = mybir.dt.bfloat16
F32 = mybir.dt.float32
U32 = mybir.dt.uint32
U8 = mybir.dt.uint8
FP8X4 = mybir.dt.float8_e4m3fn_x4

P = 128
K = 1024
N_OUT = 256
TOKENS = 8192
N_TILES = TOKENS // P
CHUNK = 4
N_CHUNKS = N_TILES // CHUNK
AHEAD = 8
GROUP = 4
T_BUFS = 4
A_BUFS = 4

FLOPS = 2 * 2 * TOKENS * K * N_OUT


def tile_virtual16bmatmul_t_kernel(tc, x, weight_upper, weight_lower, out):
    nc = tc.nc
    xf = x.flatten_outer_dims()
    of = out.flatten_outer_dims()

    with ExitStack() as ctx:
        const = ctx.enter_context(tc.tile_pool(name="const", bufs=1))
        wraw_pool = ctx.enter_context(tc.tile_pool(name="wrawp", bufs=4))
        x_pool = ctx.enter_context(tc.tile_pool(name="xp", bufs=N_CHUNKS))
        r_pool = ctx.enter_context(tc.tile_pool(name="rp", bufs=4))
        wr_pool = ctx.enter_context(tc.tile_pool(name="wrp", bufs=4))
        g_pool = ctx.enter_context(tc.tile_pool(name="gp", bufs=8))
        c_pool = ctx.enter_context(tc.tile_pool(name="cp", bufs=16))
        l_pool = ctx.enter_context(tc.tile_pool(name="lp", bufs=4))
        o_pool = ctx.enter_context(tc.tile_pool(name="op", bufs=6))
        t_psum = ctx.enter_context(tc.psum_pool(name="tps", bufs=T_BUFS))
        a_psum = ctx.enter_context(tc.psum_pool(name="aps", bufs=A_BUFS))
        ctx.enter_context(tc.manual_schedule())

        ident = const.tile([P, P], F32, name="ident")
        make_identity(nc, ident[:])

        w_raw = []
        for wi, w_src in enumerate((weight_upper, weight_lower)):
            for h in range(2):
                wr = wraw_pool.tile([P, K], BF16, name="wraw%d" % (2 * wi + h), tag="wraw")
                nc.sync.dma_start(out=wr[:], in_=w_src[P * h : P * (h + 1), :])
                w_raw.append(wr)

        x_chunks = {}

        def load_chunk(c, pieces):
            xc = x_pool.tile([P, CHUNK * K], BF16, name="xc%d" % c, tag="xc")
            src = xf[CHUNK * P * c : CHUNK * P * (c + 1), :].rearrange("(p t) k -> p (t k)", t=CHUNK)
            step = CHUNK * K // pieces
            for i in range(pieces):
                nc.sync.dma_start(out=xc[:, step * i : step * (i + 1)], in_=src[:, step * i : step * (i + 1)])
            x_chunks[c] = xc

        load_chunk(0, 4)
        load_chunk(1, 2)
        for c in range(2, AHEAD):
            load_chunk(c, 1)

        warm_src = const.tile([P, 512], BF16, name="warm_src")
        nc.vector.memset(warm_src[:], 0.0)
        warm_bank = a_psum.tile([P, 512], F32, name="warm_bank", tag="acc")

        def keep_warm(n):
            for rep in range(n):
                nc.tensor.matmul(out=warm_bank[:], lhsT=warm_src[:, 0:P], rhs=warm_src[:], start=True, stop=True)

        keep_warm(4)

        def reorder(dst, src):
            nc.vector.tensor_copy(
                out=dst.rearrange("p (u b i) -> p u b i", u=2, i=16),
                in_=src.rearrange("p (b u i) -> p u b i", u=2, i=16),
            )

        def transpose_words(bank, words, tiles, t):
            for c in range(4):
                first = (c % 2) * (2 * P * tiles) + 2 * P * t + P * (c // 2)
                nc.tensor.transpose(bank[:, c, :], words[:, first : first + P], ident[:])

        reordered = {}
        grouped = {}
        x_codes = {}
        x_scales = {}
        o_tiles = {}

        def reorder_tiles(i, n):
            t = i % CHUNK
            re = r_pool.tile([P, 2 * K], BF16, name="re%d" % i, tag="re")
            reorder(re[:, 0 : n * K], x_chunks[i // CHUNK][:, K * t : K * (t + n)])
            for s in range(n):
                reordered[i + s] = (re, n, s)

        def transpose_tile(i):
            xt = t_psum.tile([P, 4, P], F32, name="xt%d" % i, tag="xt")
            re, n, s = reordered[i]
            transpose_words(xt, re[:, 0 : n * K].bitcast(F32), n, s)
            if i < 3:
                keep_warm(1)
            gr = g_pool.tile([P, K], BF16, name="gr%d" % i, tag="gr", align_bytes=64)
            nc.scalar.copy(
                out=gr[:].bitcast(F32).rearrange("p (g r u) -> p g r u", g=2, u=2),
                in_=xt[:].rearrange("p (g u) r -> p g r u", u=2),
            )
            grouped[i] = gr

        def quantise_tile(i):
            xcod = c_pool.tile([P, K // 4], U32, name="xcod%d" % i, tag="xcod", align_bytes=64)
            xsca = c_pool.tile([P, K // 4], U8, name="xsca%d" % i, tag="xsca", align_bytes=64)
            nc.vector.quantize_mx(out=xcod[:].bitcast(FP8X4), scales=xsca[:], in_=grouped[i][:])
            x_codes[i] = xcod
            x_scales[i] = xsca

        def multiply_tile(i):
            c = i // CHUNK
            t = i % CHUNK
            last = i >= N_TILES - 2
            bank = a_psum.tile([P, 2, N_OUT], F32, name="acc%d" % i, tag="acc")
            if t == 0:
                o_tiles[c] = o_pool.tile([P, CHUNK * N_OUT], F32, name="osb%d" % c, tag="osb")
            cols = slice(N_OUT * t, N_OUT * (t + 1))
            dst = of[CHUNK * P * c : CHUNK * P * (c + 1), :].rearrange("(p t) n -> p (t n)", t=CHUNK)
            width = N_OUT if last else 2 * N_OUT
            starts = [(g, n) for g in range(2) for n in range(0, 2 * N_OUT, width)]
            for n_pass, (g, n) in enumerate(starts):
                w_cols = slice(2 * N_OUT * g + n, 2 * N_OUT * g + n + width)
                nc.tensor.matmul_mx(
                    out=bank[:].rearrange("p h n -> p (h n)")[:, 0:width],
                    lhsT=x_codes[i][:, P * g : P * (g + 1)].bitcast(FP8X4),
                    lhsT_scale=x_scales[i][:, P * g : P * (g + 1)],
                    rhs=w_codes[:, w_cols].bitcast(FP8X4),
                    rhs_scale=w_scales[:, w_cols],
                    start=(n_pass == 0),
                    stop=(n_pass == len(starts) - 1),
                )
            if last:
                (nc.scalar.copy if t % 2 == 0 else nc.vector.tensor_copy)(out=o_tiles[c][:, cols], in_=bank[:, 0, :])
                nc.sync.dma_start(out=dst[:, cols], in_=o_tiles[c][:, cols])
                return
            low = l_pool.tile([P, N_OUT], F32, name="low%d" % i, tag="low")
            nc.scalar.copy(out=low[:], in_=bank[:, 1, :])
            nc.vector.tensor_tensor(out=o_tiles[c][:, cols], in0=bank[:, 0, :], in1=low[:], op=mybir.AluOpType.add)
            if c == N_CHUNKS - 1 and t == 1:
                nc.sync.dma_start(out=dst[:, 0 : 2 * N_OUT], in_=o_tiles[c][:, 0 : 2 * N_OUT])
            elif t == CHUNK - 1:
                nc.sync.dma_start(out=dst, in_=o_tiles[c][:])
                if c + AHEAD < N_CHUNKS:
                    load_chunk(c + AHEAD, 1)

        w_re = []
        w_grouped = []
        w_codes = const.tile([P, 4 * N_OUT], U32, name="w_codes", align_bytes=64)
        w_scales = const.tile([P, 4 * N_OUT], U8, name="w_scales", align_bytes=64)
        for h in range(4):
            wre = wr_pool.tile([P, K], BF16, name="wre%d" % h, tag="wre")
            reorder(wre[:], w_raw[h][:])
            w_re.append(wre)

        def transpose_weight(wi):
            wg = const.tile([P, 4 * 2 * N_OUT], BF16, name="wg%d" % wi, align_bytes=64)
            wg_words = wg[:].bitcast(F32).rearrange("p (g n u) -> p g n u", g=2, u=2)
            for h in range(2):
                wt = t_psum.tile([P, 4, P], F32, name="wt%d" % (2 * wi + h), tag="xt")
                transpose_words(wt, w_re[2 * wi + h][:].bitcast(F32), 1, 0)
                keep_warm(1)
                (nc.vector.tensor_copy if (wi, h) == (0, 1) else nc.scalar.copy)(
                    out=wg_words[:, :, P * h : P * (h + 1), :],
                    in_=wt[:].rearrange("p (g u) r -> p g r u", u=2),
                )
            w_grouped.append(wg)

        def quantise_weight(wi):
            for g in range(2):
                w_cols = slice(N_OUT * (2 * g + wi), N_OUT * (2 * g + wi + 1))
                nc.vector.quantize_mx(
                    out=w_codes[:, w_cols].bitcast(FP8X4),
                    scales=w_scales[:, w_cols],
                    in_=w_grouped[wi][:, 4 * N_OUT * g : 4 * N_OUT * (g + 1)],
                )

        groups = [[0, 1], [2, 3]] + [list(range(s, s + GROUP)) for s in range(4, N_TILES, GROUP)]
        transpose_weight(0)
        for i in groups[0]:
            reorder_tiles(i, 1)
        transpose_weight(1)
        quantise_weight(0)
        reorder_tiles(2, 2)
        for i in groups[0]:
            transpose_tile(i)
        quantise_weight(1)
        for i in groups[0]:
            quantise_tile(i)
        for k in range(len(groups)):
            following = groups[k + 1] if k + 1 < len(groups) else []
            ahead = groups[k + 2] if k + 2 < len(groups) else []
            for i in following:
                transpose_tile(i)
            pairs = ahead[::2]
            if len(following) == GROUP:
                quantise_tile(following[0])
                for i in pairs[:1]:
                    reorder_tiles(i, 2)
                quantise_tile(following[1])
                quantise_tile(following[2])
                for i in pairs[1:]:
                    reorder_tiles(i, 2)
                quantise_tile(following[3])
            else:
                for n, i in enumerate(following):
                    for j in pairs[n : n + 1]:
                        reorder_tiles(j, 2)
                    quantise_tile(i)
            for i in groups[k]:
                multiply_tile(i)
